import numpy as np
import ml_dtypes

BF16 = ml_dtypes.bfloat16


def bf(x):
    return np.asarray(x, np.float32).astype(BF16)


def f32(x):
    return np.asarray(x, np.float32)


def f64(x):
    return np.asarray(x).astype(np.float64)


def striped(idx):
    return np.tile(idx.reshape(-1, 16).T, (8, 1))


S, D, H, O, N = 1024, 128, 256, 128, 128


def gelu_tanh(v):
    return 0.5 * v * (1.0 + np.tanh(np.sqrt(2.0 / np.pi) * (v + 0.044715 * v**3)))


def setup_inputs():
    return {"x": bf(np.random.standard_normal((D, S))), "w1": bf(np.random.standard_normal((D, H)) / np.sqrt(D)), "b1": f32(0.1 * np.random.standard_normal((H, 1))), "w2": bf(np.random.standard_normal((H, O)) / np.sqrt(H)), "b2": f32(0.1 * np.random.standard_normal((O, 1))), "offs": striped(np.random.permutation(S)[:N])}


def reference(x, w1, b1, w2, b2, offs):
    idx = offs[:16].T.reshape(-1)
    h = gelu_tanh(f64(w1).T @ f64(x)[:, idx] + f64(b1))
    return f64(w2).T @ h + f64(b2)

@@ -1,0 +1,60 @@
+import concourse.mybir as mybir
+
+BF16, F32, U16 = mybir.dt.bfloat16, mybir.dt.float32, mybir.dt.uint16
+GELU_TANH = mybir.ActivationFunctionType.Gelu_apprx_tanh
+
+P = 128
+S = 1024
+N = 128
+H = 256
+HALVES = H // P
+O = 128
+
+FLOPS = 2 * P * H * N + 2 * H * O * N
+
+
+def tile_adaptivemodalityencoder_kernel(tc, x, w1, b1, w2, b2, offs, out):
+    nc = tc.nc
+    with (
+        tc.tile_pool(name="held", bufs=1) as held,
+        tc.psum_pool(name="psum", bufs=1) as psum,
+    ):
+        offsets = held.tile([P, N // 16], U16, name="offsets")
+        nc.sync.dma_start(offsets[:], offs)
+        x_tile = held.tile([P, S], BF16, name="x_tile")
+        nc.sync.dma_start(x_tile[:], x)
+        w1_tile = held.tile([P, H], BF16, name="w1_tile")
+        nc.scalar.dma_start(w1_tile[:], w1)
+        b1_tile = held.tile([P, HALVES, 1], F32, name="b1_tile")
+        nc.scalar.dma_start(b1_tile[:], b1.rearrange("(half p) one -> p half one", p=P))
+        w2_tile = held.tile([P, HALVES, O], BF16, name="w2_tile")
+        nc.gpsimd.dma_start(w2_tile[:], w2.rearrange("(half p) o -> p half o", p=P))
+        b2_tile = held.tile([P, 1], F32, name="b2_tile")
+        nc.gpsimd.dma_start(b2_tile[:], b2)
+
+        h_tiles = []
+        for half in range(HALVES):
+            pre = psum.tile([P, N], F32, name=f"pre{half}")
+            nc.tensor.matmul(
+                pre[:],
+                w1_tile[:, half * P : (half + 1) * P],
+                x_tile[:].indirect(offsets[:]),
+                start=True,
+                stop=True,
+            )
+            h = held.tile([P, N], BF16, name=f"h{half}")
+            nc.scalar.activation(h[:], pre[:], GELU_TANH, bias=b1_tile[:, half, :])
+            h_tiles.append(h)
+
+        acc = psum.tile([P, N], F32, name="acc")
+        for half in range(HALVES):
+            nc.tensor.matmul(
+                acc[:],
+                w2_tile[:, half, :],
+                h_tiles[half][:],
+                start=(half == 0),
+                stop=(half == HALVES - 1),
+            )
+        result = held.tile([P, N], F32, name="result")
+        nc.vector.tensor_scalar_add(result[:], acc[:], b2_tile[:])
+        nc.sync.dma_start(out, result[:])

@@ -32,6 +32,10 @@ def tile_adaptivemodalityencoder_kernel(tc, x, w1, b1, w2, b2, offs, out):
         b2_tile = held.tile([P, 1], F32, name="b2_tile")
         nc.gpsimd.dma_start(b2_tile[:], b2)
 
+        warm = held.tile([P, 1], F32, name="warm")
+        nc.vector.memset(warm[:], 0.0)
+        nc.scalar.activation(warm[:], warm[:], GELU_TANH)
+
         h_tiles = []
         for half in range(HALVES):
             pre = psum.tile([P, N], F32, name=f"pre{half}")

@@ -22,15 +22,15 @@ def tile_adaptivemodalityencoder_kernel(tc, x, w1, b1, w2, b2, offs, out):
         offsets = held.tile([P, N // 16], U16, name="offsets")
         nc.sync.dma_start(offsets[:], offs)
         x_tile = held.tile([P, S], BF16, name="x_tile")
-        nc.sync.dma_start(x_tile[:], x)
+        nc.scalar.dma_start(x_tile[:], x)
         w1_tile = held.tile([P, H], BF16, name="w1_tile")
-        nc.scalar.dma_start(w1_tile[:], w1)
+        nc.sync.dma_start(w1_tile[:], w1)
         b1_tile = held.tile([P, HALVES, 1], F32, name="b1_tile")
         nc.scalar.dma_start(b1_tile[:], b1.rearrange("(half p) one -> p half one", p=P))
         w2_tile = held.tile([P, HALVES, O], BF16, name="w2_tile")
-        nc.gpsimd.dma_start(w2_tile[:], w2.rearrange("(half p) o -> p half o", p=P))
+        nc.sync.dma_start(w2_tile[:], w2.rearrange("(half p) o -> p half o", p=P))
         b2_tile = held.tile([P, 1], F32, name="b2_tile")
-        nc.gpsimd.dma_start(b2_tile[:], b2)
+        nc.sync.dma_start(b2_tile[:], b2)
 
         warm = held.tile([P, 1], F32, name="warm")
         nc.vector.memset(warm[:], 0.0)

@@ -23,42 +23,52 @@ def tile_adaptivemodalityencoder_kernel(tc, x, w1, b1, w2, b2, offs, out):
         nc.sync.dma_start(offsets[:], offs)
         x_tile = held.tile([P, S], BF16, name="x_tile")
         nc.scalar.dma_start(x_tile[:], x)
+        b1_row = held.tile([1, H], F32, name="b1_row")
+        nc.sync.dma_start(b1_row[:], b1.rearrange("m one -> one m"))
+        b2_row = held.tile([1, O], F32, name="b2_row")
+        nc.sync.dma_start(b2_row[:], b2.rearrange("o one -> one o"))
         w1_tile = held.tile([P, H], BF16, name="w1_tile")
         nc.sync.dma_start(w1_tile[:], w1)
-        b1_tile = held.tile([P, HALVES, 1], F32, name="b1_tile")
-        nc.scalar.dma_start(b1_tile[:], b1.rearrange("(half p) one -> p half one", p=P))
         w2_tile = held.tile([P, HALVES, O], BF16, name="w2_tile")
-        nc.sync.dma_start(w2_tile[:], w2.rearrange("(half p) o -> p half o", p=P))
-        b2_tile = held.tile([P, 1], F32, name="b2_tile")
-        nc.sync.dma_start(b2_tile[:], b2)
+        nc.scalar.dma_start(w2_tile[:], w2.rearrange("(half p) o -> p half o", p=P))
 
         warm = held.tile([P, 1], F32, name="warm")
         nc.vector.memset(warm[:], 0.0)
         nc.scalar.activation(warm[:], warm[:], GELU_TANH)
 
-        h_tiles = []
+        ones_row = held.tile([1, N], F32, name="ones_row")
+        nc.vector.memset(ones_row[:], 1.0)
+        pre_tiles = []
         for half in range(HALVES):
             pre = psum.tile([P, N], F32, name=f"pre{half}")
             nc.tensor.matmul(
-                pre[:],
+                pre[:], b1_row[:, half * P : (half + 1) * P], ones_row[:], start=True, stop=False
+            )
+            pre_tiles.append(pre)
+        acc = psum.tile([P, N], F32, name="acc")
+        nc.tensor.matmul(acc[:], b2_row[:], ones_row[:], start=True, stop=False)
+
+        h_tiles = []
+        for half in range(HALVES):
+            nc.tensor.matmul(
+                pre_tiles[half][:],
                 w1_tile[:, half * P : (half + 1) * P],
                 x_tile[:].indirect(offsets[:]),
-                start=True,
+                start=False,
                 stop=True,
             )
             h = held.tile([P, N], BF16, name=f"h{half}")
-            nc.scalar.activation(h[:], pre[:], GELU_TANH, bias=b1_tile[:, half, :])
+            nc.scalar.activation(h[:], pre_tiles[half][:], GELU_TANH)
             h_tiles.append(h)
 
-        acc = psum.tile([P, N], F32, name="acc")
         for half in range(HALVES):
             nc.tensor.matmul(
                 acc[:],
                 w2_tile[:, half, :],
                 h_tiles[half][:],
-                start=(half == 0),
+                start=False,
                 stop=(half == HALVES - 1),
             )
         result = held.tile([P, N], F32, name="result")
-        nc.vector.tensor_scalar_add(result[:], acc[:], b2_tile[:])
+        nc.vector.tensor_copy(result[:], acc[:])
         nc.sync.dma_start(out, result[:])

@@ -9,6 +9,8 @@ N = 128
 H = 256
 HALVES = H // P
 O = 128
+BANK = 512
+WARM_MATMULS = 4
 
 FLOPS = 2 * P * H * N + 2 * H * O * N
 
@@ -23,52 +25,46 @@ def tile_adaptivemodalityencoder_kernel(tc, x, w1, b1, w2, b2, offs, out):
         nc.sync.dma_start(offsets[:], offs)
         x_tile = held.tile([P, S], BF16, name="x_tile")
         nc.scalar.dma_start(x_tile[:], x)
-        b1_row = held.tile([1, H], F32, name="b1_row")
-        nc.sync.dma_start(b1_row[:], b1.rearrange("m one -> one m"))
-        b2_row = held.tile([1, O], F32, name="b2_row")
-        nc.sync.dma_start(b2_row[:], b2.rearrange("o one -> one o"))
         w1_tile = held.tile([P, H], BF16, name="w1_tile")
         nc.sync.dma_start(w1_tile[:], w1)
+        b1_tile = held.tile([P, HALVES, 1], F32, name="b1_tile")
+        nc.scalar.dma_start(b1_tile[:], b1.rearrange("(half p) one -> p half one", p=P))
         w2_tile = held.tile([P, HALVES, O], BF16, name="w2_tile")
-        nc.scalar.dma_start(w2_tile[:], w2.rearrange("(half p) o -> p half o", p=P))
+        nc.sync.dma_start(w2_tile[:], w2.rearrange("(half p) o -> p half o", p=P))
+        b2_tile = held.tile([P, 1], F32, name="b2_tile")
+        nc.sync.dma_start(b2_tile[:], b2)
 
-        warm = held.tile([P, 1], F32, name="warm")
-        nc.vector.memset(warm[:], 0.0)
-        nc.scalar.activation(warm[:], warm[:], GELU_TANH)
-
-        ones_row = held.tile([1, N], F32, name="ones_row")
-        nc.vector.memset(ones_row[:], 1.0)
-        pre_tiles = []
-        for half in range(HALVES):
-            pre = psum.tile([P, N], F32, name=f"pre{half}")
-            nc.tensor.matmul(
-                pre[:], b1_row[:, half * P : (half + 1) * P], ones_row[:], start=True, stop=False
-            )
-            pre_tiles.append(pre)
-        acc = psum.tile([P, N], F32, name="acc")
-        nc.tensor.matmul(acc[:], b2_row[:], ones_row[:], start=True, stop=False)
+        zeros = held.tile([P, BANK], BF16, name="zeros")
+        nc.vector.memset(zeros[:], 0.0)
+        unused_gelu = held.tile([P, 1], F32, name="unused_gelu")
+        nc.scalar.activation(unused_gelu[:], zeros[:, 0:1], GELU_TANH)
+        unused_bank = psum.tile([P, BANK], F32, name="unused_bank")
+        for repeat in range(WARM_MATMULS):
+            nc.tensor.matmul(unused_bank[:], zeros[:, 0:P], zeros[:], start=True, stop=True)
 
         h_tiles = []
         for half in range(HALVES):
+            pre = psum.tile([P, N], F32, name=f"pre{half}")
             nc.tensor.matmul(
-                pre_tiles[half][:],
+                pre[:],
                 w1_tile[:, half * P : (half + 1) * P],
                 x_tile[:].indirect(offsets[:]),
-                start=False,
+                start=True,
                 stop=True,
             )
             h = held.tile([P, N], BF16, name=f"h{half}")
-            nc.scalar.activation(h[:], pre_tiles[half][:], GELU_TANH)
+            nc.scalar.activation(h[:], pre[:], GELU_TANH, bias=b1_tile[:, half, :])
             h_tiles.append(h)
 
+        acc = psum.tile([P, N], F32, name="acc")
         for half in range(HALVES):
             nc.tensor.matmul(
                 acc[:],
                 w2_tile[:, half, :],
                 h_tiles[half][:],
-                start=False,
+                start=(half == 0),
                 stop=(half == HALVES - 1),
             )
         result = held.tile([P, N], F32, name="result")
-        nc.vector.tensor_copy(result[:], acc[:])
+        nc.vector.tensor_scalar_add(result[:], acc[:], b2_tile[:])
         nc.sync.dma_start(out, result[:])

@@ -28,9 +28,9 @@ def tile_adaptivemodalityencoder_kernel(tc, x, w1, b1, w2, b2, offs, out):
         w1_tile = held.tile([P, H], BF16, name="w1_tile")
         nc.sync.dma_start(w1_tile[:], w1)
         b1_tile = held.tile([P, HALVES, 1], F32, name="b1_tile")
-        nc.scalar.dma_start(b1_tile[:], b1.rearrange("(half p) one -> p half one", p=P))
+        nc.sync.dma_start(b1_tile[:], b1.rearrange("(half p) one -> p half one", p=P))
         w2_tile = held.tile([P, HALVES, O], BF16, name="w2_tile")
-        nc.sync.dma_start(w2_tile[:], w2.rearrange("(half p) o -> p half o", p=P))
+        nc.scalar.dma_start(w2_tile[:], w2.rearrange("(half p) o -> p half o", p=P))
         b2_tile = held.tile([P, 1], F32, name="b2_tile")
         nc.sync.dma_start(b2_tile[:], b2)
 

@@ -10,6 +10,7 @@ H = 256
 HALVES = H // P
 O = 128
 BANK = 512
+REPEATS = BANK // P
 WARM_MATMULS = 4
 
 FLOPS = 2 * P * H * N + 2 * H * O * N
@@ -34,13 +35,14 @@ def tile_adaptivemodalityencoder_kernel(tc, x, w1, b1, w2, b2, offs, out):
         b2_tile = held.tile([P, 1], F32, name="b2_tile")
         nc.sync.dma_start(b2_tile[:], b2)
 
-        zeros = held.tile([P, BANK], BF16, name="zeros")
+        zeros = held.tile([P, P], BF16, name="zeros")
         nc.vector.memset(zeros[:], 0.0)
         unused_gelu = held.tile([P, 1], F32, name="unused_gelu")
         nc.scalar.activation(unused_gelu[:], zeros[:, 0:1], GELU_TANH)
-        unused_bank = psum.tile([P, BANK], F32, name="unused_bank")
-        for repeat in range(WARM_MATMULS):
-            nc.tensor.matmul(unused_bank[:], zeros[:, 0:P], zeros[:], start=True, stop=True)
+        unused_bank = psum.tile([P, REPEATS, P], F32, name="unused_bank")
+        zeros_repeated = zeros[:].unsqueeze(1).to_broadcast([P, REPEATS, P])
+        for warm in range(WARM_MATMULS):
+            nc.tensor.matmul(unused_bank[:], zeros[:], zeros_repeated, start=True, stop=True)
 
         h_tiles = []
         for half in range(HALVES):

@@ -9,6 +9,8 @@ N = 128
 H = 256
 HALVES = H // P
 O = 128
+PIECES = 2
+PIECE = N // PIECES
 BANK = 512
 REPEATS = BANK // P
 WARM_MATMULS = 4
@@ -44,7 +46,7 @@ def tile_adaptivemodalityencoder_kernel(tc, x, w1, b1, w2, b2, offs, out):
         for warm in range(WARM_MATMULS):
             nc.tensor.matmul(unused_bank[:], zeros[:], zeros_repeated, start=True, stop=True)
 
-        h_tiles = []
+        pre_tiles = []
         for half in range(HALVES):
             pre = psum.tile([P, N], F32, name=f"pre{half}")
             nc.tensor.matmul(
@@ -54,19 +56,29 @@ def tile_adaptivemodalityencoder_kernel(tc, x, w1, b1, w2, b2, offs, out):
                 start=True,
                 stop=True,
             )
-            h = held.tile([P, N], BF16, name=f"h{half}")
-            nc.scalar.activation(h[:], pre[:], GELU_TANH, bias=b1_tile[:, half, :])
-            h_tiles.append(h)
+            pre_tiles.append(pre)
 
-        acc = psum.tile([P, N], F32, name="acc")
-        for half in range(HALVES):
-            nc.tensor.matmul(
-                acc[:],
-                w2_tile[:, half, :],
-                h_tiles[half][:],
-                start=(half == 0),
-                stop=(half == HALVES - 1),
+        pieces = [slice(piece * PIECE, (piece + 1) * PIECE) for piece in range(PIECES)]
+        h_first = held.tile([P, N], BF16, name="h_first")
+        nc.scalar.activation(h_first[:], pre_tiles[0][:], GELU_TANH, bias=b1_tile[:, 0, :])
+        h_last = []
+        for piece in range(PIECES):
+            h_piece = held.tile([P, PIECE], BF16, name=f"h_last{piece}")
+            nc.scalar.activation(
+                h_piece[:], pre_tiles[1][:, pieces[piece]], GELU_TANH, bias=b1_tile[:, 1, :]
             )
-        result = held.tile([P, N], F32, name="result")
-        nc.vector.tensor_scalar_add(result[:], acc[:], b2_tile[:])
-        nc.sync.dma_start(out, result[:])
+            h_last.append(h_piece)
+
+        acc_tiles = [psum.tile([P, PIECE], F32, name=f"acc{piece}") for piece in range(PIECES)]
+        for piece in range(PIECES):
+            nc.tensor.matmul(
+                acc_tiles[piece][:], w2_tile[:, 0, :], h_first[:, pieces[piece]], start=True, stop=False
+            )
+        for piece in range(PIECES):
+            nc.tensor.matmul(
+                acc_tiles[piece][:], w2_tile[:, 1, :], h_last[piece][:], start=False, stop=True
+            )
+        for piece in range(PIECES):
+            result = held.tile([P, PIECE], F32, name=f"result{piece}")
+            nc.vector.tensor_scalar_add(result[:], acc_tiles[piece][:], b2_tile[:])
+            nc.sync.dma_start(out[:, pieces[piece]], result[:])

@@ -30,10 +30,10 @@ def tile_adaptivemodalityencoder_kernel(tc, x, w1, b1, w2, b2, offs, out):
         nc.scalar.dma_start(x_tile[:], x)
         w1_tile = held.tile([P, H], BF16, name="w1_tile")
         nc.sync.dma_start(w1_tile[:], w1)
-        b1_tile = held.tile([P, HALVES, 1], F32, name="b1_tile")
-        nc.sync.dma_start(b1_tile[:], b1.rearrange("(half p) one -> p half one", p=P))
+        b1_tile = held.tile([P, HALVES], F32, name="b1_tile")
+        nc.sync.dma_start(b1_tile[:], b1.rearrange("(p half) one -> p (half one)", half=HALVES))
         w2_tile = held.tile([P, HALVES, O], BF16, name="w2_tile")
-        nc.scalar.dma_start(w2_tile[:], w2.rearrange("(half p) o -> p half o", p=P))
+        nc.scalar.dma_start(w2_tile[:], w2.rearrange("(p half) o -> p half o", half=HALVES))
         b2_tile = held.tile([P, 1], F32, name="b2_tile")
         nc.sync.dma_start(b2_tile[:], b2)
 
@@ -51,7 +51,7 @@ def tile_adaptivemodalityencoder_kernel(tc, x, w1, b1, w2, b2, offs, out):
             pre = psum.tile([P, N], F32, name=f"pre{half}")
             nc.tensor.matmul(
                 pre[:],
-                w1_tile[:, half * P : (half + 1) * P],
+                w1_tile[:, half::HALVES],
                 x_tile[:].indirect(offsets[:]),
                 start=True,
                 stop=True,
@@ -60,12 +60,12 @@ def tile_adaptivemodalityencoder_kernel(tc, x, w1, b1, w2, b2, offs, out):
 
         pieces = [slice(piece * PIECE, (piece + 1) * PIECE) for piece in range(PIECES)]
         h_first = held.tile([P, N], BF16, name="h_first")
-        nc.scalar.activation(h_first[:], pre_tiles[0][:], GELU_TANH, bias=b1_tile[:, 0, :])
+        nc.scalar.activation(h_first[:], pre_tiles[0][:], GELU_TANH, bias=b1_tile[:, 0:1])
         h_last = []
         for piece in range(PIECES):
             h_piece = held.tile([P, PIECE], BF16, name=f"h_last{piece}")
             nc.scalar.activation(
-                h_piece[:], pre_tiles[1][:, pieces[piece]], GELU_TANH, bias=b1_tile[:, 1, :]
+                h_piece[:], pre_tiles[1][:, pieces[piece]], GELU_TANH, bias=b1_tile[:, 1:2]
             )
             h_last.append(h_piece)
 

@@ -46,26 +46,25 @@ def tile_adaptivemodalityencoder_kernel(tc, x, w1, b1, w2, b2, offs, out):
         for warm in range(WARM_MATMULS):
             nc.tensor.matmul(unused_bank[:], zeros[:], zeros_repeated, start=True, stop=True)
 
-        pre_tiles = []
-        for half in range(HALVES):
-            pre = psum.tile([P, N], F32, name=f"pre{half}")
+        pre_first = psum.tile([P, N], F32, name="pre_first")
+        nc.tensor.matmul(
+            pre_first[:], w1_tile[:, 0::HALVES], x_tile[:].indirect(offsets[:]), start=True, stop=True
+        )
+        pre_last = [psum.tile([P, PIECE], F32, name=f"pre_last{piece}") for piece in range(PIECES)]
+        for piece in range(PIECES):
+            piece_offsets = offsets[:, piece * PIECE // 16 : (piece + 1) * PIECE // 16]
             nc.tensor.matmul(
-                pre[:],
-                w1_tile[:, half::HALVES],
-                x_tile[:].indirect(offsets[:]),
-                start=True,
-                stop=True,
+                pre_last[piece][:], w1_tile[:, 1::HALVES], x_tile[:].indirect(piece_offsets), start=True, stop=True
             )
-            pre_tiles.append(pre)
 
         pieces = [slice(piece * PIECE, (piece + 1) * PIECE) for piece in range(PIECES)]
         h_first = held.tile([P, N], BF16, name="h_first")
-        nc.scalar.activation(h_first[:], pre_tiles[0][:], GELU_TANH, bias=b1_tile[:, 0:1])
+        nc.scalar.activation(h_first[:], pre_first[:], GELU_TANH, bias=b1_tile[:, 0:1])
         h_last = []
         for piece in range(PIECES):
             h_piece = held.tile([P, PIECE], BF16, name=f"h_last{piece}")
             nc.scalar.activation(
-                h_piece[:], pre_tiles[1][:, pieces[piece]], GELU_TANH, bias=b1_tile[:, 1:2]
+                h_piece[:], pre_last[piece][:], GELU_TANH, bias=b1_tile[:, 1:2]
             )
             h_last.append(h_piece)
 

@@ -24,12 +24,12 @@ def tile_adaptivemodalityencoder_kernel(tc, x, w1, b1, w2, b2, offs, out):
         tc.tile_pool(name="held", bufs=1) as held,
         tc.psum_pool(name="psum", bufs=1) as psum,
     ):
+        x_tile = held.tile([P, S], BF16, name="x_tile")
+        nc.sync.dma_start(x_tile[:], x)
+        w1_tile = held.tile([P, H], BF16, name="w1_tile")
+        nc.scalar.dma_start(w1_tile[:], w1)
         offsets = held.tile([P, N // 16], U16, name="offsets")
         nc.sync.dma_start(offsets[:], offs)
-        x_tile = held.tile([P, S], BF16, name="x_tile")
-        nc.scalar.dma_start(x_tile[:], x)
-        w1_tile = held.tile([P, H], BF16, name="w1_tile")
-        nc.sync.dma_start(w1_tile[:], w1)
         b1_tile = held.tile([P, HALVES], F32, name="b1_tile")
         nc.sync.dma_start(b1_tile[:], b1.rearrange("(p half) one -> p (half one)", half=HALVES))
         w2_tile = held.tile([P, HALVES, O], BF16, name="w2_tile")

@@ -13,7 +13,7 @@ PIECES = 2
 PIECE = N // PIECES
 BANK = 512
 REPEATS = BANK // P
-WARM_MATMULS = 4
+WARM_MATMULS = 3
 
 FLOPS = 2 * P * H * N + 2 * H * O * N
 

@@ -31,9 +31,9 @@ def tile_adaptivemodalityencoder_kernel(tc, x, w1, b1, w2, b2, offs, out):
         offsets = held.tile([P, N // 16], U16, name="offsets")
         nc.sync.dma_start(offsets[:], offs)
         b1_tile = held.tile([P, HALVES], F32, name="b1_tile")
-        nc.sync.dma_start(b1_tile[:], b1.rearrange("(p half) one -> p (half one)", half=HALVES))
+        nc.scalar.dma_start(b1_tile[:], b1.rearrange("(p half) one -> p (half one)", half=HALVES))
         w2_tile = held.tile([P, HALVES, O], BF16, name="w2_tile")
-        nc.scalar.dma_start(w2_tile[:], w2.rearrange("(p half) o -> p half o", half=HALVES))
+        nc.sync.dma_start(w2_tile[:], w2.rearrange("(p half) o -> p half o", half=HALVES))
         b2_tile = held.tile([P, 1], F32, name="b2_tile")
         nc.sync.dma_start(b2_tile[:], b2)
 

@@ -46,37 +46,31 @@ def tile_adaptivemodalityencoder_kernel(tc, x, w1, b1, w2, b2, offs, out):
         for warm in range(WARM_MATMULS):
             nc.tensor.matmul(unused_bank[:], zeros[:], zeros_repeated, start=True, stop=True)
 
-        pre_first = psum.tile([P, N], F32, name="pre_first")
-        nc.tensor.matmul(
-            pre_first[:], w1_tile[:, 0::HALVES], x_tile[:].indirect(offsets[:]), start=True, stop=True
-        )
-        pre_last = [psum.tile([P, PIECE], F32, name=f"pre_last{piece}") for piece in range(PIECES)]
+        pieces = [slice(piece * PIECE, (piece + 1) * PIECE) for piece in range(PIECES)]
+        h_tiles = []
         for piece in range(PIECES):
             piece_offsets = offsets[:, piece * PIECE // 16 : (piece + 1) * PIECE // 16]
-            nc.tensor.matmul(
-                pre_last[piece][:], w1_tile[:, 1::HALVES], x_tile[:].indirect(piece_offsets), start=True, stop=True
-            )
+            for half in range(HALVES):
+                pre = psum.tile([P, PIECE], F32, name=f"pre{piece}{half}")
+                nc.tensor.matmul(
+                    pre[:], w1_tile[:, half::HALVES], x_tile[:].indirect(piece_offsets), start=True, stop=True
+                )
+                h_tile = held.tile([P, PIECE], BF16, name=f"h{piece}{half}")
+                nc.scalar.activation(h_tile[:], pre[:], GELU_TANH, bias=b1_tile[:, half : half + 1])
+                h_tiles.append(h_tile)
 
-        pieces = [slice(piece * PIECE, (piece + 1) * PIECE) for piece in range(PIECES)]
-        h_first = held.tile([P, N], BF16, name="h_first")
-        nc.scalar.activation(h_first[:], pre_first[:], GELU_TANH, bias=b1_tile[:, 0:1])
-        h_last = []
+        acc_tiles = []
         for piece in range(PIECES):
-            h_piece = held.tile([P, PIECE], BF16, name=f"h_last{piece}")
-            nc.scalar.activation(
-                h_piece[:], pre_last[piece][:], GELU_TANH, bias=b1_tile[:, 1:2]
-            )
-            h_last.append(h_piece)
-
-        acc_tiles = [psum.tile([P, PIECE], F32, name=f"acc{piece}") for piece in range(PIECES)]
-        for piece in range(PIECES):
-            nc.tensor.matmul(
-                acc_tiles[piece][:], w2_tile[:, 0, :], h_first[:, pieces[piece]], start=True, stop=False
-            )
-        for piece in range(PIECES):
-            nc.tensor.matmul(
-                acc_tiles[piece][:], w2_tile[:, 1, :], h_last[piece][:], start=False, stop=True
-            )
+            acc = psum.tile([P, PIECE], F32, name=f"acc{piece}")
+            for half in range(HALVES):
+                nc.tensor.matmul(
+                    acc[:],
+                    w2_tile[:, half, :],
+                    h_tiles[piece * HALVES + half][:],
+                    start=half == 0,
+                    stop=half == HALVES - 1,
+                )
+            acc_tiles.append(acc)
         for piece in range(PIECES):
             result = held.tile([P, PIECE], F32, name=f"result{piece}")
             nc.vector.tensor_scalar_add(result[:], acc_tiles[piece][:], b2_tile[:])

import concourse.mybir as mybir

BF16, F32, U16 = mybir.dt.bfloat16, mybir.dt.float32, mybir.dt.uint16
GELU_TANH = mybir.ActivationFunctionType.Gelu_apprx_tanh

P = 128
S = 1024
N = 128
H = 256
HALVES = H // P
O = 128
PIECES = 2
PIECE = N // PIECES
BANK = 512
REPEATS = BANK // P
WARM_MATMULS = 3

FLOPS = 2 * P * H * N + 2 * H * O * N


def tile_adaptivemodalityencoder_kernel(tc, x, w1, b1, w2, b2, offs, out):
    nc = tc.nc
    with (
        tc.tile_pool(name="held", bufs=1) as held,
        tc.psum_pool(name="psum", bufs=1) as psum,
    ):
        x_tile = held.tile([P, S], BF16, name="x_tile")
        nc.sync.dma_start(x_tile[:], x)
        w1_tile = held.tile([P, H], BF16, name="w1_tile")
        nc.scalar.dma_start(w1_tile[:], w1)
        offsets = held.tile([P, N // 16], U16, name="offsets")
        nc.sync.dma_start(offsets[:], offs)
        b1_tile = held.tile([P, HALVES], F32, name="b1_tile")
        nc.scalar.dma_start(b1_tile[:], b1.rearrange("(p half) one -> p (half one)", half=HALVES))
        w2_tile = held.tile([P, HALVES, O], BF16, name="w2_tile")
        nc.sync.dma_start(w2_tile[:], w2.rearrange("(p half) o -> p half o", half=HALVES))
        b2_tile = held.tile([P, 1], F32, name="b2_tile")
        nc.sync.dma_start(b2_tile[:], b2)

        zeros = held.tile([P, P], BF16, name="zeros")
        nc.vector.memset(zeros[:], 0.0)
        unused_gelu = held.tile([P, 1], F32, name="unused_gelu")
        nc.scalar.activation(unused_gelu[:], zeros[:, 0:1], GELU_TANH)
        unused_bank = psum.tile([P, REPEATS, P], F32, name="unused_bank")
        zeros_repeated = zeros[:].unsqueeze(1).to_broadcast([P, REPEATS, P])
        for warm in range(WARM_MATMULS):
            nc.tensor.matmul(unused_bank[:], zeros[:], zeros_repeated, start=True, stop=True)

        pieces = [slice(piece * PIECE, (piece + 1) * PIECE) for piece in range(PIECES)]
        h_tiles = []
        for piece in range(PIECES):
            piece_offsets = offsets[:, piece * PIECE // 16 : (piece + 1) * PIECE // 16]
            for half in range(HALVES):
                pre = psum.tile([P, PIECE], F32, name=f"pre{piece}{half}")
                nc.tensor.matmul(
                    pre[:], w1_tile[:, half::HALVES], x_tile[:].indirect(piece_offsets), start=True, stop=True
                )
                h_tile = held.tile([P, PIECE], BF16, name=f"h{piece}{half}")
                nc.scalar.activation(h_tile[:], pre[:], GELU_TANH, bias=b1_tile[:, half : half + 1])
                h_tiles.append(h_tile)

        acc_tiles = []
        for piece in range(PIECES):
            acc = psum.tile([P, PIECE], F32, name=f"acc{piece}")
            for half in range(HALVES):
                nc.tensor.matmul(
                    acc[:],
                    w2_tile[:, half, :],
                    h_tiles[piece * HALVES + half][:],
                    start=half == 0,
                    stop=half == HALVES - 1,
                )
            acc_tiles.append(acc)
        for piece in range(PIECES):
            result = held.tile([P, PIECE], F32, name=f"result{piece}")
            nc.vector.tensor_scalar_add(result[:], acc_tiles[piece][:], b2_tile[:])
            nc.sync.dma_start(out[:, pieces[piece]], result[:])
